import numpy as np
import ml_dtypes


def mxq(x, axis, fmt="e4m3"):
    dtype, down = {"e4m3": (ml_dtypes.float8_e4m3fn, 7), "e5m2": (ml_dtypes.float8_e5m2, 14)}[fmt]
    v = np.moveaxis(np.asarray(x, np.float32).astype(ml_dtypes.bfloat16).astype(np.float64), axis, -1)
    blocks = v.reshape(v.shape[:-1] + (-1, 32))
    amax = np.abs(blocks).max(-1, keepdims=True)
    byte = np.maximum(np.where(amax > 0, np.frexp(amax)[1] - 1 + 127, 0) - down, 1)
    scale = np.exp2(byte - 127.0)
    codes = (blocks / scale).astype(np.float32).astype(dtype).astype(np.float64)
    return np.moveaxis((codes * scale).reshape(v.shape), -1, axis)


WIDE = False


def mx_kscale(k):
    if not WIDE:
        return np.ones(k)
    levels = np.array([10, -10, 5, -5, 0])
    if k % 512:
        return np.exp2(np.random.permutation(np.resize(levels, k // 32))).repeat(32)
    a = np.empty((k // 512, 16))
    for p in range(k // 512):
        a[p, :8] = np.random.permutation(np.resize(levels, 8))
        for g in range(8):
            far = levels[np.abs(levels - a[p, g]) >= 10]
            a[p, g + 8] = far[np.random.randint(len(far))]
    return np.exp2(a.ravel()).repeat(32)


BF16 = ml_dtypes.bfloat16


def bf(x):
    return np.asarray(x, np.float32).astype(BF16)


def f64(x):
    return np.asarray(x).astype(np.float64)


E2M1 = np.array([0.0, 0.5, 1.0, 1.5, 2.0, 3.0, 4.0, 6.0, -0.0, -0.5, -1.0, -1.5, -2.0, -3.0, -4.0, -6.0])


def pack_weight(w, fmt):
    k, n = w.shape
    w = f64(bf(w)).reshape(k // 32, 32, n)
    amax = np.abs(w).max(1)
    if fmt == "e4m3":
        byte = np.frexp(amax)[1] - 1 + 127 - 7
    else:
        mant, ex = np.frexp(amax / 6.0)
        byte = np.where(mant > 0.5, ex, ex - 1) + 127
    byte = np.clip(np.where(amax > 0, byte, 1), 1, 254)
    scaled = (w * np.exp2(127.0 - byte)[:, None, :]).reshape(k, n).astype(np.float32)
    by_word = np.ascontiguousarray(scaled.reshape(k // 512, 128, 4, n).transpose(0, 1, 3, 2))
    if fmt == "e4m3":
        words = by_word.astype(ml_dtypes.float8_e4m3fn).view(np.uint8)
    else:
        c = by_word.astype(ml_dtypes.float4_e2m1fn).view(np.uint8) & 0xF
        words = c[..., 0::2] | (c[..., 1::2] << 4)
    return np.ascontiguousarray(words), np.ascontiguousarray(byte.astype(np.uint8).reshape(k // 512, 16, n))


def unpack_weight(words, scales, fmt):
    g, p, n, _ = words.shape
    if fmt == "e4m3":
        vals = np.ascontiguousarray(words).view(ml_dtypes.float8_e4m3fn).astype(np.float64)
    else:
        nib = np.empty((g, p, n, 4), np.uint8)
        nib[..., 0::2] = words & 0xF
        nib[..., 1::2] = words >> 4
        vals = E2M1[nib]
    vals = vals * np.repeat(np.exp2(scales.astype(np.float64) - 127.0), 8, axis=1)[..., None]
    return vals.transpose(0, 1, 3, 2).reshape(g * 512, n)


B, DIM, E, HID = 1024, 1024, 1024, 2048
EPS = 1e-5


def layer_norm(y, g, b):
    m = y.mean(-1, keepdims=True)
    v = ((y - m) ** 2).mean(-1, keepdims=True)
    return (y - m) / np.sqrt(v + EPS) * g + b


def draw0():
    s, t = mx_kscale(DIM), mx_kscale(E)
    r = np.random.standard_normal
    feat = bf(r((B, DIM)))
    own_self = bf(r((B, DIM)))
    other_self = bf(r((B, DIM)) * s)
    Wv_words, Wv_scales = pack_weight((r((E, DIM)) / np.sqrt(DIM) / s[None, :] * t[:, None]).T, 'e4m3')
    bv = bf(r(E) * 0.2 * t)
    Wo_words, Wo_scales = pack_weight((r((DIM, E)) / np.sqrt(E) / t[None, :]).T, 'e4m3')
    return {'feat': feat,
            'own_self': own_self,
            'other_self': other_self,
            'Wv_words': Wv_words,
            'Wv_scales': Wv_scales,
            'bv': bv,
            'Wo_words': Wo_words,
            'Wo_scales': Wo_scales,
            'bo': bf(r(DIM) * 0.2),
            'g': bf(1.0 + 0.1 * r(DIM)),
            'be': bf(0.1 * r(DIM))}


def core(feat, own_self, other_self, Wv_words, Wv_scales, bv, Wo_words, Wo_scales, bo, g, be):
    val = (mxq(f64(other_self), 1, 'e4m3') @ unpack_weight(Wv_words, Wv_scales, 'e4m3')) + f64(bv)
    cross = (mxq(val, 1, 'e4m3') @ unpack_weight(Wo_words, Wo_scales, 'e4m3')) + f64(bo)
    return layer_norm(f64(feat) + (f64(own_self) + cross) * 0.5, f64(g), f64(be))


def e4m3fn_bytes(y):
    return np.clip(np.asarray(y, np.float64), -448.0, 448.0).astype(np.float32).astype(ml_dtypes.float8_e4m3fn).view(np.uint8)


def e4m3fn_values(b):
    return np.asarray(b, np.uint8).view(ml_dtypes.float8_e4m3fn).astype(np.float64)


def setup_inputs():
    d = draw0()
    x0 = np.asarray(d['other_self']).astype(np.float64)
    s = (np.max(np.abs(x0), axis=(0,), keepdims=True) / 448.0).astype(np.float32)
    out = {}
    for k, v in d.items():
        if k == 'other_self':
            out['other_self_bytes'] = e4m3fn_bytes(x0 / s.astype(np.float64))
            out['other_self_scale'] = s
        else:
            out[k] = v
    return out


def reference(feat, own_self, other_self_bytes, other_self_scale, Wv_words, Wv_scales, bv, Wo_words, Wo_scales, bo, g, be):
    return core(feat, own_self, e4m3fn_values(other_self_bytes) * other_self_scale.astype(np.float64), Wv_words, Wv_scales, bv, Wo_words, Wo_scales, bo, g, be)

from contextlib import ExitStack

import concourse.mybir as mybir
from concourse.masks import make_identity

F32 = mybir.dt.float32
BF16 = mybir.dt.bfloat16
I32 = mybir.dt.int32
U32 = mybir.dt.uint32
U8 = mybir.dt.uint8
FP8 = mybir.dt.float8_e4m3fn
FP8X4 = mybir.dt.float8_e4m3fn_x4
ADD = mybir.AluOpType.add
MULT = mybir.AluOpType.mult
ACT = mybir.ActivationFunctionType

P = 128
B, D = 1024, 1024
TILES = B // P
H = 512
EPS = 1e-5
FLOPS = 2 * 2 * B * D * D

PE_HALVES = {(0, 0), (0, 1), (5, 0), (5, 1), (6, 0), (6, 1), (7, 0)}
G_STEP = {0: [1], 1: [2], 2: [3], 3: [4], 4: [7]}


def tile_efficientfusionlayer_pb_w8_kernel(
    tc, feat, own_self, x_bytes, x_scale, wv_words, wv_scales, bv, wo_words, wo_scales, bo, g, be, out
):
    nc = tc.nc
    feat_v = feat.rearrange("(p i) n -> p i n", i=TILES)
    own_v = own_self.rearrange("(p i) n -> p i n", i=TILES)
    x_v = x_bytes.rearrange("(p i) n -> p i n", i=TILES)
    out_v = out.rearrange("(p i) n -> p i n", i=TILES)

    with ExitStack() as ctx:
        keep = ctx.enter_context(tc.tile_pool(name="keep", bufs=1))
        pipe = ctx.enter_context(tc.tile_pool(name="pipe", bufs=3))
        psum = ctx.enter_context(tc.psum_pool(name="psum", bufs=1))
        ctx.enter_context(tc.manual_schedule())

        warm = keep.tile([P, 1], F32)
        nc.vector.memset(warm[:], 1.0)
        warm2 = keep.tile([P, 1], F32)
        nc.scalar.activation(out=warm2[:], in_=warm[:], func=ACT.Abs_reciprocal_sqrt, bias=warm[:, 0:1], scale=1.0)
        eps = keep.tile([P, 1], F32)
        nc.vector.memset(eps[:], EPS)
        wvs_raw = keep.tile([P, D], U8, align_bytes=64)
        nc.vector.memset(wvs_raw[:].bitcast(I32), 0)
        wos = keep.tile([P, D], U8, align_bytes=64)
        nc.vector.memset(wos[:].bitcast(I32), 0)
        rows = keep.tile([P, D], BF16)
        nc.vector.memset(rows[:], 0.0)

        ident_f = keep.tile([P, P], F32)
        make_identity(nc, ident_f[:])
        ident_b = keep.tile([P, P], BF16)
        make_identity(nc, ident_b[:])

        x_bytes_tiles = []
        for c in range(TILES // 2):
            x_held = keep.tile([P, 2, D], U8, name=f"x_held{c}")
            x_bytes_tiles.append(x_held)
        own_tiles = []
        feat_tiles = []
        for c in range(TILES // 2):
            own_t = keep.tile([P, 2, D], BF16, name=f"own{c}")
            own_tiles.append(own_t)
            feat_t = keep.tile([P, 2, D], BF16, name=f"feat{c}")
            feat_tiles.append(feat_t)
        xs = keep.tile([P, 2, 4], F32)
        bv_h = keep.tile([P, 2, 4], BF16)
        wv_raw = keep.tile([P, 2, D], I32, align_bytes=64)
        wo = keep.tile([P, 2, D], I32, align_bytes=64)
        bo_b = keep.tile([P, D], BF16)
        be_b = keep.tile([P, D], BF16)

        nc.sync.dma_start(out=x_bytes_tiles[0][:], in_=x_v[:, 0:2, :])
        nc.scalar.dma_start(out=xs[:], in_=x_scale.rearrange("o (g p t) -> p (o g) t", p=P, t=4))
        nc.scalar.dma_start(out=bv_h[:], in_=bv.rearrange("(g p t) -> p g t", p=P, t=4))
        for q in range(4):
            nc.sync.dma_start(
                out=wvs_raw[32 * q : 32 * q + 8, :].bitcast(I32), in_=wv_scales[:, 4 * q : 4 * q + 4, :].bitcast(I32)
            )
        for c in range(2):
            nc.sync.dma_start(
                out=wv_raw[:, c, :], in_=wv_words[c].rearrange("p n t -> p (n t)").bitcast(I32)
            )
        for c in range(1, TILES // 2):
            nc.sync.dma_start(out=x_bytes_tiles[c][:], in_=x_v[:, 2 * c : 2 * c + 2, :])
        for q in range(4):
            nc.sync.dma_start(
                out=wos[32 * q : 32 * q + 8, :].bitcast(I32), in_=wo_scales[:, 4 * q : 4 * q + 4, :].bitcast(I32)
            )
        nc.sync.dma_start(out=rows[0:1, :], in_=g.rearrange("(o n) -> o n", o=1))
        nc.sync.dma_start(out=rows[1:2, :], in_=bo.rearrange("(o n) -> o n", o=1))
        for c in range(2):
            nc.sync.dma_start(out=wo[:, c, :], in_=wo_words[c].rearrange("p n t -> p (n t)").bitcast(I32))
        nc.sync.dma_start(out=bo_b[:], in_=bo.partition_broadcast(P))
        for c in range(TILES // 2):
            nc.sync.dma_start(out=own_tiles[c][:], in_=own_v[:, 2 * c : 2 * c + 2, :])
            nc.sync.dma_start(out=feat_tiles[c][:], in_=feat_v[:, 2 * c : 2 * c + 2, :])
            if c == 1:
                nc.sync.dma_start(out=be_b[:], in_=be.partition_broadcast(P))

        half_b = keep.tile([P, P], BF16)
        nc.vector.tensor_scalar(out=half_b[:], in0=ident_b[:], scalar1=0.5, scalar2=None, op0=MULT)
        bv_f = keep.tile([P, 2, 4], F32)
        nc.vector.tensor_copy(out=bv_f[:], in_=bv_h[:])
        bo_h = keep.tile([P, D], BF16)
        wv = keep.tile([P, 2, D], I32, align_bytes=64)
        wvs = keep.tile([P, D], U8, align_bytes=64)
        g_ps = psum.tile([P, D], BF16)

        def permute_wv():
            nc.vector.tensor_copy(
                out=wvs[:].rearrange("p (v t c) -> p v c t", v=2, t=4),
                in_=wvs_raw[:].rearrange("p (v c t) -> p v c t", v=2, t=4),
            )
            for v in range(2):
                for c in range(2):
                    cols = slice(v * H, (v + 1) * H)
                    nc.vector.tensor_copy(
                        out=wv[:, c, cols].rearrange("p (t c i) -> p c t i", t=4, i=4),
                        in_=wv_raw[:, c, cols].rearrange("p (c i t) -> p c t i", t=4, i=4),
                    )

        xw, xps, xg, xq, xqs = {}, {}, {}, {}, {}
        vps, vg, vq, vqs = {}, {}, {}, {}
        cps, res, ys, sums, zs = {}, {}, {}, {}, {}

        def widen(i):
            x_wide = pipe.tile([P, D], BF16)
            xw[i] = x_wide
            nc.scalar.copy(out=x_wide[:], in_=x_bytes_tiles[i // 2][:, i % 2, :].bitcast(FP8))

        def turn(i):
            x_ps = psum.tile([P, 4, P], F32, bufs=2)
            xps[i] = x_ps
            words = xw[i][:].bitcast(F32)
            for c in range(2):
                for u in range(2):
                    nc.tensor.transpose(x_ps[:, 2 * c + u, :], words[:, 256 * c + u : 256 * (c + 1) : 2], ident_f[:])

        def scale_x(i):
            x_grouped = pipe.tile([P, 2, H], BF16, align_bytes=64)
            xg[i] = x_grouped
            pairs = xps[i][:].rearrange("p a r -> p (a r)").bitcast(BF16)
            pairs = pairs.rearrange("p (c u r e) -> p c r u e", c=2, u=2, e=2)
            for c in range(2):
                nc.vector.tensor_tensor(
                    out=x_grouped[:, c, :].rearrange("p (r u e) -> p r u e", u=2, e=2),
                    in0=pairs[:, c],
                    in1=xs[:, c, :].rearrange("p (u e) -> p u e", u=2).unsqueeze(1).to_broadcast([P, P, 2, 2]),
                    op=MULT,
                )

        def quant_x(i):
            x_codes = pipe.tile([P, 2 * P], U32, align_bytes=64)
            x_planes = pipe.tile([P, 2 * P], U8, align_bytes=64)
            xq[i], xqs[i] = x_codes, x_planes
            nc.vector.quantize_mx(
                out=x_codes[:].bitcast(FP8X4), scales=x_planes[:], in_=xg[i][:].rearrange("p c n -> p (c n)")
            )

        def stage1(i):
            for v in range(2):
                v_ps = psum.tile([P, 4, P], F32, bufs=2)
                vps[i, v] = v_ps
                for t in range(4):
                    cols = slice(v * H + t * P, v * H + (t + 1) * P)
                    for c in range(2):
                        nc.tensor.matmul_mx(
                            out=v_ps[:, t, :],
                            lhsT=wv[:, c, cols].bitcast(FP8X4),
                            lhsT_scale=wvs[4 * c : P, cols],
                            rhs=xq[i][:, c * P : (c + 1) * P].bitcast(FP8X4),
                            rhs_scale=xqs[i][:, c * P : (c + 1) * P],
                            start=(c == 0),
                            stop=(c == 1),
                        )

        def val_out(i):
            v_grouped = pipe.tile([P, 2, H], BF16, align_bytes=64)
            vg[i] = v_grouped
            for v in range(2):
                nc.vector.tensor_tensor(
                    out=v_grouped[:, v, :].rearrange("p (r t) -> p r t", t=4),
                    in0=vps[i, v][:].rearrange("p t r -> p r t"),
                    in1=bv_f[:, v, :].unsqueeze(1).to_broadcast([P, P, 4]),
                    op=ADD,
                )

        def quant_v(i):
            v_codes = pipe.tile([P, 2 * P], U32, align_bytes=64)
            v_planes = pipe.tile([P, 2 * P], U8, align_bytes=64)
            vq[i], vqs[i] = v_codes, v_planes
            nc.vector.quantize_mx(
                out=v_codes[:].bitcast(FP8X4), scales=v_planes[:], in_=vg[i][:].rearrange("p c n -> p (c n)")
            )

        def stage2(i):
            for h in range(2):
                c_ps = psum.tile([P, H], F32, bufs=2)
                cps[i, h] = c_ps
                cols = slice(h * H, (h + 1) * H)
                for c in range(2):
                    nc.tensor.matmul_mx(
                        out=c_ps[:],
                        lhsT=vq[i][:, c * P : (c + 1) * P].bitcast(FP8X4),
                        lhsT_scale=vqs[i][:, c * P : (c + 1) * P],
                        rhs=wo[:, c, cols].bitcast(FP8X4),
                        rhs_scale=wos[4 * c : P, cols],
                        start=(c == 0),
                        stop=(c == 1),
                    )

        def res_tile(i):
            if i not in res:
                residual = pipe.tile([P, D], F32, bufs=6)
                res[i] = residual
            return res[i]

        def res_pe(i, h):
            residual = res_tile(i)
            cols = slice(h * H, (h + 1) * H)
            r_ps = psum.tile([P, H], F32)
            nc.tensor.matmul(r_ps[:], lhsT=half_b[:], rhs=own_tiles[i // 2][:, i % 2, cols], start=True, stop=False)
            nc.tensor.matmul(r_ps[:], lhsT=ident_b[:], rhs=feat_tiles[i // 2][:, i % 2, cols], start=False, stop=False)
            nc.tensor.matmul(
                r_ps[:], lhsT=half_b[:, 1:2].to_broadcast([P, P]), rhs=rows[:, cols], start=False, stop=True
            )
            nc.scalar.copy(out=residual[:, cols], in_=r_ps[:])

        def res_g(i):
            residual = res_tile(i)
            lo = H if (i, 0) in PE_HALVES else 0
            own_half = pipe.tile([P, D], BF16)
            nc.vector.tensor_scalar(
                out=own_half[:, lo:D], in0=own_tiles[i // 2][:, i % 2, lo:D], scalar1=0.5, scalar2=None, op0=MULT
            )
            part = pipe.tile([P, D], F32)
            for c0 in range(lo, D, H):
                cols = slice(c0, c0 + H)
                nc.gpsimd.tensor_tensor(out=part[:, cols], in0=own_half[:, cols], in1=bo_h[:, cols], op=ADD)
                nc.gpsimd.tensor_tensor(
                    out=residual[:, cols], in0=feat_tiles[i // 2][:, i % 2, cols], in1=part[:, cols], op=ADD
                )

        def y_out(i):
            y = pipe.tile([P, D], F32)
            y_sums = pipe.tile([P, 2], F32)
            ys[i], sums[i] = y, y_sums
            for h in range(2):
                cols = slice(h * H, (h + 1) * H)
                nc.vector.scalar_tensor_tensor(
                    out=y[:, cols],
                    in0=cps[i, h][:],
                    scalar=0.5,
                    in1=res[i][:, cols],
                    op0=MULT,
                    op1=ADD,
                    accum_out=y_sums[:, h : h + 1],
                )

        def norm(i):
            y = ys[i]
            neg_parts = pipe.tile([P, 2], F32)
            neg_mean = pipe.tile([P, 1], F32)
            nc.scalar.activation(
                out=neg_parts[:], in_=sums[i][:], func=ACT.Identity, scale=-1.0 / D, accum_out=neg_mean[:]
            )
            squares = pipe.tile([P, D], BF16)
            sq_sum = pipe.tile([P, 1], F32)
            nc.scalar.activation(
                out=squares[:], in_=y[:], func=ACT.Square, bias=neg_mean[:, 0:1], scale=1.0, accum_out=sq_sum[:]
            )
            rstd = pipe.tile([P, 1], F32)
            nc.scalar.activation(
                out=rstd[:], in_=sq_sum[:], func=ACT.Abs_reciprocal_sqrt, bias=eps[:, 0:1], scale=1.0 / D
            )
            shift = pipe.tile([P, 1], F32)
            nc.scalar.activation(out=shift[:], in_=neg_mean[:], func=ACT.Copy, scale=rstd[:, 0:1])
            z = pipe.tile([P, D], F32)
            zs[i] = z
            nc.scalar.activation(out=z[:], in_=y[:], func=ACT.Identity, bias=shift[:, 0:1], scale=rstd[:, 0:1])

        def gain_shift(i):
            scaled = pipe.tile([P, D], F32)
            nc.vector.tensor_tensor(out=scaled[:], in0=zs[i][:], in1=g_ps[:], op=MULT)
            final = pipe.tile([P, D], F32)
            engine = nc.vector if i == TILES - 1 else nc.gpsimd
            for h in range(2):
                cols = slice(h * H, (h + 1) * H)
                engine.tensor_tensor(out=final[:, cols], in0=scaled[:, cols], in1=be_b[:, cols], op=ADD)
                nc.sync.dma_start(out=out_v[:, i, cols], in_=final[:, cols])

        def live(i):
            return 0 <= i < TILES

        widen(0)
        turn(0)
        widen(1)
        for k in range(-2, TILES + 2):
            if live(k + 4):
                widen(k + 4)
            if live(k + 3):
                turn(k + 3)
            if live(k + 2):
                scale_x(k + 2)
            if k == -2:
                permute_wv()
            if live(k + 1):
                val_out(k + 1)
            if live(k + 2):
                quant_x(k + 2)
                stage1(k + 2)
            if k == -1:
                nc.vector.tensor_scalar(out=bo_h[:], in0=bo_b[:], scalar1=0.5, scalar2=None, op0=MULT)
                for h in range(2):
                    cols = slice(h * H, (h + 1) * H)
                    nc.tensor.matmul(
                        g_ps[:, cols], lhsT=ident_b[:, 0:1].to_broadcast([P, P]), rhs=rows[:, cols], start=True, stop=True
                    )
            for h in range(2):
                if (k + 1, h) in PE_HALVES:
                    res_pe(k + 1, h)
            for i in G_STEP.get(k + 1, []):
                res_g(i)
            if live(k):
                y_out(k)
                norm(k)
            if live(k + 1):
                quant_v(k + 1)
                stage2(k + 1)
            if live(k - 2):
                gain_shift(k - 2)
